import numpy as np
import ml_dtypes


def mxq(x, axis, fmt="e4m3"):
    dtype, down = {"e4m3": (ml_dtypes.float8_e4m3fn, 7), "e5m2": (ml_dtypes.float8_e5m2, 14)}[fmt]
    v = np.moveaxis(np.asarray(x, np.float32).astype(ml_dtypes.bfloat16).astype(np.float64), axis, -1)
    blocks = v.reshape(v.shape[:-1] + (-1, 32))
    amax = np.abs(blocks).max(-1, keepdims=True)
    byte = np.maximum(np.where(amax > 0, np.frexp(amax)[1] - 1 + 127, 0) - down, 1)
    scale = np.exp2(byte - 127.0)
    codes = (blocks / scale).astype(np.float32).astype(dtype).astype(np.float64)
    return np.moveaxis((codes * scale).reshape(v.shape), -1, axis)


WIDE = False


def mx_kscale(k):
    if not WIDE:
        return np.ones(k)
    levels = np.array([10, -10, 5, -5, 0])
    if k % 512:
        return np.exp2(np.random.permutation(np.resize(levels, k // 32))).repeat(32)
    a = np.empty((k // 512, 16))
    for p in range(k // 512):
        a[p, :8] = np.random.permutation(np.resize(levels, 8))
        for g in range(8):
            far = levels[np.abs(levels - a[p, g]) >= 10]
            a[p, g + 8] = far[np.random.randint(len(far))]
    return np.exp2(a.ravel()).repeat(32)


BF16 = ml_dtypes.bfloat16


def bf(x):
    return np.asarray(x, np.float32).astype(BF16)


def f64(x):
    return np.asarray(x).astype(np.float64)


B, A, S, F = 4096, 3, 128, 512


def setup_inputs():
    s, u = mx_kscale(F), mx_kscale(F)
    t, v = mx_kscale(F), mx_kscale(F)
    return {
        "h1": bf(np.maximum(np.random.standard_normal((B, A, F)) * 1.4, 0.0) * s),
        "W2": bf(np.random.standard_normal((A, F, F)) * 1.4 / np.sqrt(F) / s[:, None] * t),
        "b2": bf(np.random.standard_normal((A, F)) * 0.2 * t),
        "W3": bf(np.random.standard_normal((A, F, S)) / np.sqrt(F) / t[:, None]),
        "b3": bf(np.random.standard_normal((A, S)) * 0.2),
        "g1": bf(np.maximum(np.random.standard_normal((B, F)) * 1.4, 0.0) * u),
        "V2": bf(np.random.standard_normal((F, F)) * 1.4 / np.sqrt(F) / u[:, None] * v),
        "c2": bf(np.random.standard_normal(F) * 0.2 * v),
        "V3": bf(np.random.standard_normal((F, S)) / np.sqrt(F) / v[:, None]),
        "c3": bf(np.random.standard_normal(S) * 0.2),
    }


def reference(h1, W2, b2, W3, b3, g1, V2, c2, V3, c3):
    ha = mxq(f64(h1), 2, "e4m3").transpose(1, 0, 2)
    h2 = np.maximum((ha @ mxq(f64(W2), 1, "e4m3")) + f64(b2)[:, None, :], 0.0)
    psi_adv = ((mxq(h2, 2, "e4m3") @ mxq(f64(W3), 1, "e4m3")) + f64(b3)[:, None, :]).transpose(1, 0, 2)
    g2 = np.maximum((mxq(f64(g1), 1, "e4m3") @ mxq(f64(V2), 0, "e4m3")) + f64(c2), 0.0)
    psi_state = (mxq(g2, 1, "e4m3") @ mxq(f64(V3), 0, "e4m3")) + f64(c3)
    return psi_state[:, None, :] + psi_adv - psi_adv.mean(axis=1, keepdims=True)

@@ -1,0 +1,427 @@
+from contextlib import ExitStack
+
+import concourse.mybir as mybir
+from concourse.masks import make_identity
+
+F32 = mybir.dt.float32
+BF16 = mybir.dt.bfloat16
+U32 = mybir.dt.uint32
+U8 = mybir.dt.uint8
+FP8X4 = mybir.dt.float8_e4m3fn_x4
+ACT = mybir.ActivationFunctionType
+ALU = mybir.AluOpType
+
+P = 128
+B, A, S, F = 4096, 3, 128, 512
+NS = A + 1
+ORDER = (3, 0, 1, 2)
+ROUNDS = (512, 512, 512, 512, 512, 512, 512, 256, 256)
+NR = len(ROUNDS)
+NU = NR * NS
+FLOPS = 2 * NS * B * (F * F + F * S)
+
+LEAD_B = 3
+LEAD_C = 2
+FULL_EVERY = 2
+V_SHARE = 2
+
+
+def tile_psicritic_pa_t_kernel(tc, h1, W2, b2, W3, b3, g1, V2, c2, V3, c3, out):
+    nc = tc.nc
+    base = [sum(ROUNDS[:r]) for r in range(NR)]
+    with ExitStack() as ctx:
+        const = ctx.enter_context(tc.tile_pool(name="const", bufs=1))
+        wst = ctx.enter_context(tc.tile_pool(name="wst", bufs=2))
+        xin = ctx.enter_context(tc.tile_pool(name="xin", bufs=3))
+        xqp = ctx.enter_context(tc.tile_pool(name="xqp", bufs=4))
+        hpp = ctx.enter_context(tc.tile_pool(name="hpp", bufs=3))
+        hcp = ctx.enter_context(tc.tile_pool(name="hcp", bufs=2))
+        outp = ctx.enter_context(tc.tile_pool(name="outp", bufs=2))
+        ps_x = ctx.enter_context(tc.psum_pool(name="ps_x", bufs=2))
+        ps_h = ctx.enter_context(tc.psum_pool(name="ps_h", bufs=4))
+        ps_o = ctx.enter_context(tc.psum_pool(name="ps_o", bufs=2))
+
+        ident = const.tile([P, P], F32, name="ident")
+        make_identity(nc, ident[:])
+        ones = const.tile([P, P], BF16, name="ones")
+        nc.vector.memset(ones[:], 1.0)
+        warm = const.tile([P, 16], BF16, name="warm")
+        nc.scalar.activation(out=warm[:, 0:1], in_=ones[:, 0:1], func=ACT.Relu)
+        bz = const.tile([P, 32], BF16, name="bz")
+        zrow = const.tile([P, 4 * S], BF16, name="zrow")
+        nc.vector.memset(zrow[:], 0.0)
+
+        w2c = const.tile([P, NS * F], U32, name="w2c", align_bytes=64)
+        w2s = const.tile([P, NS * F], U8, name="w2s", align_bytes=64)
+        w3c = const.tile([P, 8 * S], U32, name="w3c", align_bytes=64)
+        w3s = const.tile([P, 8 * S], U8, name="w3s", align_bytes=64)
+        beta = const.tile([P, A * S], F32, name="beta")
+
+        xh = {}
+        xg = {}
+
+        def chunks(r):
+            return ROUNDS[r] // P
+
+        def is_full(r, j):
+            return ROUNDS[r] == 512 and (j < 2 or (j == 2 and r < 4))
+
+        def load_g(r, parts=1):
+            nj = chunks(r)
+            xg[r] = xin.tile([P, nj * F], BF16, name="xg", tag="xg")
+            rows = g1[base[r] : base[r] + ROUNDS[r], :].rearrange("(p j) k -> p j k", j=nj)
+            step = nj // parts
+            for i in range(parts):
+                nc.sync.dma_start(
+                    out=xg[r][:, F * step * i : F * step * (i + 1)].rearrange("p (j k) -> p j k", k=F),
+                    in_=rows[:, step * i : step * (i + 1), :],
+                )
+
+        def load_h(r, whole):
+            nj = chunks(r)
+            xh[r] = xin.tile([P, nj * A * F], BF16, name="xh", tag="xh")
+            if whole:
+                rows = h1[base[r] : base[r] + ROUNDS[r]]
+                nc.sync.dma_start(out=xh[r][:], in_=rows.rearrange("(p j) a k -> p (j a k)", j=nj))
+
+        def load_h_part(r, a):
+            nj = chunks(r)
+            rows = h1[base[r] : base[r] + ROUNDS[r], a : a + 1, :]
+            nc.sync.dma_start(
+                out=xh[r][:].rearrange("p (j a k) -> p j a k", j=nj, a=A)[:, :, a : a + 1, :],
+                in_=rows.rearrange("(p j) o k -> p j o k", j=nj),
+            )
+
+        w2raw = {}
+
+        def load_w2(s):
+            w2raw[s] = wst.tile([P, 4 * F], BF16, name="w2raw", tag="w2raw", bufs=4)
+            src = V2.rearrange("(p j) n -> p (j n)", j=4) if s == 3 else W2[s : s + 1].rearrange(
+                "o (p j) n -> p (o j n)", j=4
+            )
+            nc.sync.dma_start(out=w2raw[s][:], in_=src)
+
+        def prep_w2(s):
+            wg = wst.tile([P, 4 * F], BF16, name="wg", tag="wg", align_bytes=64)
+            dst = wg[:].rearrange("p (t m j) -> p t m j", t=4, j=4)
+            src = w2raw[s][:].rearrange("p (j m t) -> p t m j", t=4, j=4)
+            nc.vector.tensor_copy(out=dst, in_=src)
+            return wg
+
+        def quant_w2(s, wg):
+            nc.vector.quantize_mx(
+                out=w2c[:, F * s : F * (s + 1)].bitcast(FP8X4),
+                scales=w2s[:, F * s : F * (s + 1)],
+                in_=wg[:],
+            )
+
+        load_g(0, 2)
+        load_w2(3)
+        nc.scalar.dma_start(out=bz[:, 16:20], in_=c2.rearrange("(p t) -> p t", t=4))
+        nc.scalar.dma_start(out=bz[:, 0:12].rearrange("p (a t) -> p a t", a=A), in_=b2.rearrange("a (p t) -> p a t", t=4))
+        nc.scalar.dma_start(out=zrow[0:1, 0 : A * S], in_=b3.rearrange("(o a) s -> o (a s)", o=1))
+        nc.scalar.dma_start(out=zrow[0:1, A * S :], in_=c3.rearrange("(o s) -> o s", o=1))
+        load_h(0, False)
+        load_h_part(0, 0)
+        load_w2(0)
+        load_h_part(0, 1)
+        load_w2(1)
+        load_h_part(0, 2)
+        load_g(1)
+        load_w2(2)
+        load_h(1, True)
+        w3raw = const.tile([P, NS * 4 * S], BF16, name="w3raw")
+        nc.sync.dma_start(
+            out=w3raw[:, 0 : A * 4 * S].rearrange("p (a x) -> p a x", a=A),
+            in_=W3.rearrange("a (p t) n -> p a (t n)", t=4),
+        )
+        nc.sync.dma_start(
+            out=w3raw[:, A * 4 * S :],
+            in_=V3.rearrange("(p t) n -> p (t n)", t=4),
+        )
+        load_g(2)
+        load_h(2, True)
+
+        xt = {}
+        xq = {}
+        xc = {}
+        hps = {}
+        hp = {}
+        hq = {}
+        hc = {}
+        ops = {}
+        osb = {}
+        esb = {}
+
+        def unit(u):
+            return u // NS, ORDER[u % NS]
+
+        def halves(u):
+            return (chunks(u // NS) + 1) // 2
+
+        def b_on_vector(u, hf):
+            return V_SHARE > 0 and hf == 1 and 2 <= u < 26 and u % V_SHARE == 0
+
+        def st_a(u, hf):
+            r, s = unit(u)
+            nj = min(2, chunks(r) - 2 * hf)
+            x32 = (xg[r] if s == 3 else xh[r])[:].bitcast(F32)
+            xt[u, hf] = ps_x.tile([P, 512], F32, name="xt", tag="xt")
+            for uu in range(2):
+                for jj in range(nj):
+                    j = 2 * hf + jj
+                    col = j * 256 if s == 3 else (j * A + s) * 256
+                    nc.tensor.transpose(
+                        xt[u, hf][:, (nj * uu + jj) * P : (nj * uu + jj + 1) * P],
+                        x32[:, col + uu : col + 256 : 2],
+                        ident[:],
+                    )
+
+        def st_b(u, hf):
+            r, s = unit(u)
+            nj = min(2, chunks(r) - 2 * hf)
+            if hf == 0:
+                xq[u] = xqp.tile([P, 4 * ROUNDS[r]], BF16, name="xq", tag="xq", align_bytes=64)
+            dst = xq[u][:].bitcast(F32).rearrange("p (w u) -> p w u", u=2)[:, 256 * hf : 256 * hf + P * nj, :]
+            src = xt[u, hf][:, 0 : 2 * P * nj].rearrange("p (u w) -> p w u", u=2)
+            if b_on_vector(u, hf):
+                nc.vector.tensor_copy(out=dst, in_=src)
+            else:
+                nc.scalar.copy(out=dst, in_=src)
+
+        def st_c(u):
+            n_tok = ROUNDS[u // NS]
+            codes = xqp.tile([P, n_tok], U32, name="xc", tag="xc", align_bytes=64)
+            scales = xqp.tile([P, n_tok], U8, name="xs", tag="xs", align_bytes=64)
+            xc[u] = (codes, scales)
+            nc.vector.quantize_mx(out=codes[:].bitcast(FP8X4), scales=scales[:], in_=xq[u][:])
+
+        def st_d(u, t):
+            r, s = unit(u)
+            hps[u, t] = ps_h.tile([P, 512], F32, name="hps", tag="hps")
+            col = F * s + P * t
+            nc.tensor.matmul_mx(
+                out=hps[u, t][:, 0 : ROUNDS[r]],
+                lhsT=w2c[:, col : col + P].bitcast(FP8X4),
+                lhsT_scale=w2s[:, col : col + P],
+                rhs=xc[u][0][:].bitcast(FP8X4),
+                rhs_scale=xc[u][1][:],
+                start=True,
+                stop=True,
+            )
+
+        def st_e(u, t):
+            r, s = unit(u)
+            n_tok = ROUNDS[r]
+            if t == 0:
+                hp[u] = hpp.tile([P, 4 * n_tok], BF16, name="hp", tag="hp")
+            nc.scalar.activation(
+                out=hp[u][:, n_tok * t : n_tok * (t + 1)],
+                in_=hps[u, t][:, 0:n_tok],
+                func=ACT.Relu,
+                bias=bz[:, 4 * (4 if s == 3 else s) + t : 4 * (4 if s == 3 else s) + t + 1],
+                scale=1.0,
+            )
+
+        def st_f(u):
+            hq[u] = hpp.tile([P, 4 * ROUNDS[u // NS]], BF16, name="hq", tag="hq", align_bytes=64)
+            nc.vector.tensor_copy(
+                out=hq[u][:].rearrange("p (c i t) -> p c t i", i=4, t=4),
+                in_=hp[u][:].rearrange("p (t c i) -> p c t i", t=4, i=4),
+            )
+
+        def st_g(u):
+            r, s = unit(u)
+            codes = hcp.tile([P, ROUNDS[r]], U32, name="hc%d" % s, tag="hc%d" % s, align_bytes=64)
+            scales = hcp.tile([P, ROUNDS[r]], U8, name="hs%d" % s, tag="hs%d" % s, align_bytes=64)
+            hc[r, s] = (codes, scales)
+            nc.vector.quantize_mx(out=codes[:].bitcast(FP8X4), scales=scales[:], in_=hq[u][:])
+
+        def l2_pass(dst, r, s, j, blk, start, stop):
+            nc.tensor.matmul_mx(
+                out=dst,
+                lhsT=hc[r, s][0][:, P * j : P * (j + 1)].bitcast(FP8X4),
+                lhsT_scale=hc[r, s][1][:, P * j : P * (j + 1)],
+                rhs=w3c[:, S * blk : S * (blk + 1)].bitcast(FP8X4),
+                rhs_scale=w3s[:, S * blk : S * (blk + 1)],
+                start=start,
+                stop=stop,
+            )
+
+        def st_h(r, j):
+            ops[r, j] = ps_o.tile([P, 4 * S], F32, name="ops", tag="ops")
+            for a in range(A):
+                dst = ops[r, j][:, S * a : S * (a + 1)]
+                if is_full(r, j):
+                    l2_pass(dst, r, 3, j, 3, True, False)
+                    l2_pass(dst, r, 3, j, 7, False, False)
+                    for b in range(A):
+                        l2_pass(dst, r, b, j, b if b == a else 4 + b, False, b == A - 1)
+                else:
+                    l2_pass(dst, r, 3, j, 3, True, False)
+                    l2_pass(dst, r, a, j, a, False, True)
+            if not is_full(r, j):
+                for a in range(A):
+                    l2_pass(ops[r, j][:, S * A :], r, a, j, 4 + a, a == 0, a == A - 1)
+
+        def st_i1(r, j):
+            if is_full(r, j):
+                return
+            esb[r, j] = outp.tile([P, A * S], F32, name="esb", tag="esb")
+            nc.vector.scalar_tensor_tensor(
+                out=esb[r, j][:].rearrange("p (a s) -> p a s", a=A),
+                in0=ops[r, j][:, S * A :].unsqueeze(1).to_broadcast([P, A, S]),
+                scalar=1.0 / 3.0,
+                in1=beta[:].rearrange("p (a s) -> p a s", a=A),
+                op0=ALU.mult,
+                op1=ALU.add,
+            )
+
+        def st_i2(r, j):
+            nj = chunks(r)
+            if j == 0:
+                osb[r] = outp.tile([P, nj * A * S], F32, name="osb", tag="osb")
+            full = is_full(r, j)
+            nc.vector.scalar_tensor_tensor(
+                out=osb[r][:, A * S * j : A * S * (j + 1)],
+                in0=ops[r, j][:, 0 : A * S],
+                scalar=1.0 / 3.0 if full else 0.5,
+                in1=beta[:] if full else esb[r, j][:],
+                op0=ALU.mult,
+                op1=ALU.add,
+            )
+            if j == nj - 1:
+                rows = out[base[r] : base[r] + ROUNDS[r]]
+                nc.sync.dma_start(out=rows.rearrange("(p j) a s -> p (j a s)", j=nj), in_=osb[r][:])
+
+        def setup_beta():
+            pb = ps_o.tile([P, 4 * S], F32, name="pb", tag="ops")
+            nc.tensor.matmul(out=pb[:], lhsT=ones[:], rhs=zrow[:], start=True, stop=True)
+            bb = const.tile([P, 4 * S], F32, name="bb")
+            nc.vector.tensor_copy(out=bb[:], in_=pb[:])
+            m1 = const.tile([P, S], F32, name="m1")
+            nc.vector.tensor_tensor(out=m1[:], in0=bb[:, 0:S], in1=bb[:, S : 2 * S], op=ALU.add)
+            m2 = const.tile([P, S], F32, name="m2")
+            nc.vector.tensor_tensor(out=m2[:], in0=m1[:], in1=bb[:, 2 * S : 3 * S], op=ALU.add)
+            gm = const.tile([P, S], F32, name="gm")
+            nc.vector.scalar_tensor_tensor(
+                out=gm[:], in0=m2[:], scalar=-1.0 / 3.0, in1=bb[:, 3 * S :], op0=ALU.mult, op1=ALU.add
+            )
+            nc.vector.tensor_tensor(
+                out=beta[:].rearrange("p (a s) -> p a s", a=A),
+                in0=bb[:, 0 : A * S].rearrange("p (a s) -> p a s", a=A),
+                in1=gm[:].unsqueeze(1).to_broadcast([P, A, S]),
+                op=ALU.add,
+            )
+
+        def setup_w3():
+            w3g = const.tile([P, 8 * 4 * S], BF16, name="w3g", align_bytes=64)
+            for lo, hi, src_lo, factor in ((0, 4, 0, 2.0), (4, 7, 0, -1.0), (7, 8, 3, 1.0)):
+                nc.gpsimd.tensor_scalar(
+                    out=w3g[:, 4 * S * lo : 4 * S * hi].rearrange("p (s n t) -> p s n t", s=hi - lo, t=4),
+                    in0=w3raw[:, 4 * S * src_lo : 4 * S * (src_lo + hi - lo)].rearrange(
+                        "p (s t n) -> p s n t", s=hi - lo, t=4
+                    ),
+                    scalar1=factor,
+                    scalar2=0.0,
+                    op0=ALU.mult,
+                    op1=ALU.add,
+                )
+            return w3g
+
+        state = {"a": 0, "b": 0, "c": 0, "h": 0, "i": 0}
+        ready = []
+        h_done = []
+        seen = {}
+        n_chunks = B // P
+
+        def b_unit(u):
+            nxt = state["a"]
+            for hf in range(2):
+                if hf < halves(u):
+                    st_b(u, hf)
+                if nxt < NU and hf < halves(nxt):
+                    st_a(nxt, hf)
+            state["a"] += 1
+            state["b"] = u + 1
+
+        def quantise_h(u, n):
+            st_g(u)
+            r = u // NS
+            seen[r] = seen.get(r, 0) + 1
+            if seen[r] == NS:
+                for j in range(chunks(r)):
+                    ready.append((r, j, n))
+
+        def try_h(n, force):
+            if state["h"] < len(ready) and (force or ready[state["h"]][2] <= n - 1):
+                r, j = ready[state["h"]][0:2]
+                state["h"] += 1
+                st_h(r, j)
+                h_done.append((r, j, n))
+
+        def pop_i(n, force):
+            if state["i"] < len(h_done) and (force or h_done[state["i"]][2] <= n - 1):
+                state["i"] += 1
+                return h_done[state["i"] - 1]
+            return None
+
+        st_a(0, 0)
+        st_a(0, 1)
+        state["a"] = 1
+        quant_w2(3, prep_w2(3))
+        b_unit(0)
+        st_c(0)
+        state["c"] = 1
+        for t in range(4):
+            st_d(0, t)
+        pending = {0: prep_w2(0)}
+        b_unit(1)
+        for n in range(NU + 1):
+            if n >= 2 and n % NS == 2 and n // NS + 3 < NR:
+                load_g(n // NS + 3)
+                load_h(n // NS + 3, True)
+            while state["c"] < NU and state["c"] <= n + LEAD_C and state["c"] < state["b"]:
+                st_c(state["c"])
+                state["c"] += 1
+                if n < 2:
+                    break
+            if n == 0:
+                quant_w2(0, pending[0])
+                pending[1] = prep_w2(1)
+            if n == 1:
+                quant_w2(1, pending[1])
+                pending[2] = prep_w2(2)
+            if n == 2:
+                quant_w2(2, pending[2])
+                pending[3] = setup_w3()
+                setup_beta()
+            if n == 4:
+                nc.vector.quantize_mx(out=w3c[:].bitcast(FP8X4), scales=w3s[:], in_=pending[3][:])
+            late = n >= NU - 2 * NS
+            chunk = pop_i(n, late)
+            if n < NU:
+                for t in range(4):
+                    st_e(n, t)
+                    if n + 1 < NU:
+                        st_d(n + 1, t)
+            try_h(n, late)
+            if n >= 1:
+                st_f(n - 1)
+            count = 0
+            while state["b"] < NU and state["b"] <= n + (2 if n < 3 else LEAD_B) and count < 2:
+                b_unit(state["b"])
+                count += 1
+            if chunk:
+                st_i1(chunk[0], chunk[1])
+            if n >= 1:
+                quantise_h(n - 1, n)
+            if chunk:
+                st_i2(chunk[0], chunk[1])
+        while state["i"] < n_chunks:
+            try_h(NU, True)
+            try_h(NU, True)
+            while state["i"] < len(h_done):
+                chunk = pop_i(NU, True)
+                st_i1(chunk[0], chunk[1])
+                st_i2(chunk[0], chunk[1])

@@ -20,10 +20,8 @@ NR = len(ROUNDS)
 NU = NR * NS
 FLOPS = 2 * NS * B * (F * F + F * S)
 
-LEAD_B = 3
-LEAD_C = 2
-FULL_EVERY = 2
-V_SHARE = 2
+V_COPIES = 8
+ENGINES = {mybir.EngineType.PE, mybir.EngineType.Activation, mybir.EngineType.DVE}
 
 
 def tile_psicritic_pa_t_kernel(tc, h1, W2, b2, W3, b3, g1, V2, c2, V3, c3, out):
@@ -35,8 +33,9 @@ def tile_psicritic_pa_t_kernel(tc, h1, W2, b2, W3, b3, g1, V2, c2, V3, c3, out):
         xin = ctx.enter_context(tc.tile_pool(name="xin", bufs=3))
         xqp = ctx.enter_context(tc.tile_pool(name="xqp", bufs=4))
         hpp = ctx.enter_context(tc.tile_pool(name="hpp", bufs=3))
-        hcp = ctx.enter_context(tc.tile_pool(name="hcp", bufs=2))
-        outp = ctx.enter_context(tc.tile_pool(name="outp", bufs=2))
+        hcp = ctx.enter_context(tc.tile_pool(name="hcp", bufs=3))
+        outp = ctx.enter_context(tc.tile_pool(name="outp", bufs=3))
+        pinned = tc.manual_schedule(engines=ENGINES)
         ps_x = ctx.enter_context(tc.psum_pool(name="ps_x", bufs=2))
         ps_h = ctx.enter_context(tc.psum_pool(name="ps_h", bufs=4))
         ps_o = ctx.enter_context(tc.psum_pool(name="ps_o", bufs=2))
@@ -64,7 +63,7 @@ def tile_psicritic_pa_t_kernel(tc, h1, W2, b2, W3, b3, g1, V2, c2, V3, c3, out):
             return ROUNDS[r] // P
 
         def is_full(r, j):
-            return ROUNDS[r] == 512 and (j < 2 or (j == 2 and r < 4))
+            return ROUNDS[r] == 512 and j % 2 == 0
 
         def load_g(r, parts=1):
             nj = chunks(r)
@@ -160,7 +159,7 @@ def tile_psicritic_pa_t_kernel(tc, h1, W2, b2, W3, b3, g1, V2, c2, V3, c3, out):
             return (chunks(u // NS) + 1) // 2
 
         def b_on_vector(u, hf):
-            return V_SHARE > 0 and hf == 1 and 2 <= u < 26 and u % V_SHARE == 0
+            return hf == 1 and u % V_COPIES == 2
 
         def st_a(u, hf):
             r, s = unit(u)
@@ -329,99 +328,96 @@ def tile_psicritic_pa_t_kernel(tc, h1, W2, b2, W3, b3, g1, V2, c2, V3, c3, out):
                 )
             return w3g
 
-        state = {"a": 0, "b": 0, "c": 0, "h": 0, "i": 0}
         ready = []
         h_done = []
-        seen = {}
-        n_chunks = B // P
-
-        def b_unit(u):
-            nxt = state["a"]
-            for hf in range(2):
-                if hf < halves(u):
-                    st_b(u, hf)
-                if nxt < NU and hf < halves(nxt):
-                    st_a(nxt, hf)
-            state["a"] += 1
-            state["b"] = u + 1
+        state = {"h": 0, "i": 0}
 
         def quantise_h(u, n):
             st_g(u)
-            r = u // NS
-            seen[r] = seen.get(r, 0) + 1
-            if seen[r] == NS:
-                for j in range(chunks(r)):
-                    ready.append((r, j, n))
+            if u % NS == NS - 1:
+                for j in range(chunks(u // NS)):
+                    ready.append((u // NS, j, n))
 
-        def try_h(n, force):
-            if state["h"] < len(ready) and (force or ready[state["h"]][2] <= n - 1):
+        def try_h(n):
+            if state["h"] < len(ready) and ready[state["h"]][2] <= n - 1:
                 r, j = ready[state["h"]][0:2]
                 state["h"] += 1
                 st_h(r, j)
                 h_done.append((r, j, n))
 
-        def pop_i(n, force):
-            if state["i"] < len(h_done) and (force or h_done[state["i"]][2] <= n - 1):
+        def pop_i(n):
+            if state["i"] < len(h_done) and h_done[state["i"]][2] <= n - 1:
                 state["i"] += 1
                 return h_done[state["i"] - 1]
             return None
 
-        st_a(0, 0)
-        st_a(0, 1)
-        state["a"] = 1
-        quant_w2(3, prep_w2(3))
-        b_unit(0)
+        def both_a(u):
+            for hf in range(halves(u)):
+                st_a(u, hf)
+
+        def both_b(u, vector):
+            for hf in range(halves(u)):
+                if b_on_vector(u, hf) == vector:
+                    st_b(u, hf)
+
+        ctx.enter_context(pinned)
+        both_a(0)
+        wg3 = prep_w2(3)
+        both_b(0, False)
+        both_a(1)
+        quant_w2(3, wg3)
         st_c(0)
-        state["c"] = 1
         for t in range(4):
             st_d(0, t)
-        pending = {0: prep_w2(0)}
-        b_unit(1)
+        both_b(1, False)
+        both_a(2)
+        wg0 = prep_w2(0)
+        st_c(1)
+        quant_w2(0, wg0)
+        both_b(2, False)
+        both_b(2, True)
+        later = {0: prep_w2(1), 1: None, 2: None}
+        w3g = setup_w3()
         for n in range(NU + 1):
-            if n >= 2 and n % NS == 2 and n // NS + 3 < NR:
+            if n + 3 < NU:
+                both_a(n + 3)
+            if n % NS == 0 and n // NS + 3 < NR:
                 load_g(n // NS + 3)
                 load_h(n // NS + 3, True)
-            while state["c"] < NU and state["c"] <= n + LEAD_C and state["c"] < state["b"]:
-                st_c(state["c"])
-                state["c"] += 1
-                if n < 2:
-                    break
-            if n == 0:
-                quant_w2(0, pending[0])
-                pending[1] = prep_w2(1)
-            if n == 1:
-                quant_w2(1, pending[1])
-                pending[2] = prep_w2(2)
-            if n == 2:
-                quant_w2(2, pending[2])
-                pending[3] = setup_w3()
-                setup_beta()
-            if n == 4:
-                nc.vector.quantize_mx(out=w3c[:].bitcast(FP8X4), scales=w3s[:], in_=pending[3][:])
-            late = n >= NU - 2 * NS
-            chunk = pop_i(n, late)
-            if n < NU:
-                for t in range(4):
+            try_h(n)
+            for t in range(4):
+                if n < NU:
                     st_e(n, t)
-                    if n + 1 < NU:
-                        st_d(n + 1, t)
-            try_h(n, late)
+                if n + 1 < NU:
+                    st_d(n + 1, t)
+            if n + 3 < NU:
+                both_b(n + 3, False)
+            chunk = pop_i(n)
             if n >= 1:
                 st_f(n - 1)
-            count = 0
-            while state["b"] < NU and state["b"] <= n + (2 if n < 3 else LEAD_B) and count < 2:
-                b_unit(state["b"])
-                count += 1
+            if n + 2 < NU:
+                st_c(n + 2)
+            if n < 2:
+                quant_w2(n + 1, later[n])
+            if n == 0:
+                later[1] = prep_w2(2)
+            if n == 2:
+                setup_beta()
             if chunk:
                 st_i1(chunk[0], chunk[1])
             if n >= 1:
                 quantise_h(n - 1, n)
             if chunk:
                 st_i2(chunk[0], chunk[1])
-        while state["i"] < n_chunks:
-            try_h(NU, True)
-            try_h(NU, True)
-            while state["i"] < len(h_done):
-                chunk = pop_i(NU, True)
+            if n + 3 < NU:
+                both_b(n + 3, True)
+            if n == 4:
+                nc.vector.quantize_mx(out=w3c[:].bitcast(FP8X4), scales=w3s[:], in_=w3g[:])
+        n = NU + 1
+        while state["i"] < B // P:
+            try_h(n)
+            chunk = pop_i(n)
+            if chunk:
                 st_i1(chunk[0], chunk[1])
                 st_i2(chunk[0], chunk[1])
+            n += 1

@@ -42,10 +42,12 @@ def tile_psicritic_pa_t_kernel(tc, h1, W2, b2, W3, b3, g1, V2, c2, V3, c3, out):
 
         ident = const.tile([P, P], F32, name="ident")
         make_identity(nc, ident[:])
-        ones = const.tile([P, P], BF16, name="ones")
-        nc.vector.memset(ones[:], 1.0)
+        threes = const.tile([P, P], BF16, name="threes")
+        nc.vector.memset(threes[:], 3.0)
+        minus = const.tile([P, P], BF16, name="minus")
+        nc.vector.memset(minus[:], -1.0)
         warm = const.tile([P, 16], BF16, name="warm")
-        nc.scalar.activation(out=warm[:, 0:1], in_=ones[:, 0:1], func=ACT.Relu)
+        nc.scalar.activation(out=warm[:, 0:1], in_=threes[:, 0:1], func=ACT.Relu)
         bz = const.tile([P, 32], BF16, name="bz")
         zrow = const.tile([P, 4 * S], BF16, name="zrow")
         nc.vector.memset(zrow[:], 0.0)
@@ -63,7 +65,7 @@ def tile_psicritic_pa_t_kernel(tc, h1, W2, b2, W3, b3, g1, V2, c2, V3, c3, out):
             return ROUNDS[r] // P
 
         def is_full(r, j):
-            return ROUNDS[r] == 512 and j % 2 == 0
+            return r == NR - 1 or (ROUNDS[r] == 512 and j % 2 == 0)
 
         def load_g(r, parts=1):
             nj = chunks(r)
@@ -76,19 +78,20 @@ def tile_psicritic_pa_t_kernel(tc, h1, W2, b2, W3, b3, g1, V2, c2, V3, c3, out):
                     in_=rows[:, step * i : step * (i + 1), :],
                 )
 
-        def load_h(r, whole):
+        def load_h(r):
             nj = chunks(r)
             xh[r] = xin.tile([P, nj * A * F], BF16, name="xh", tag="xh")
-            if whole:
-                rows = h1[base[r] : base[r] + ROUNDS[r]]
-                nc.sync.dma_start(out=xh[r][:], in_=rows.rearrange("(p j) a k -> p (j a k)", j=nj))
+            rows = h1[base[r] : base[r] + ROUNDS[r]]
+            nc.sync.dma_start(out=xh[r][:], in_=rows.rearrange("(p j) a k -> p (j a k)", j=nj))
 
-        def load_h_part(r, a):
-            nj = chunks(r)
-            rows = h1[base[r] : base[r] + ROUNDS[r], a : a + 1, :]
+        h_first = {}
+
+        def load_h_first(a):
+            nj = chunks(0)
+            h_first[a] = const.tile([P, nj * F], BF16, name="h_first%d" % a)
             nc.sync.dma_start(
-                out=xh[r][:].rearrange("p (j a k) -> p j a k", j=nj, a=A)[:, :, a : a + 1, :],
-                in_=rows.rearrange("(p j) o k -> p j o k", j=nj),
+                out=h_first[a][:].rearrange("p (j k) -> p j k", j=nj),
+                in_=h1[0 : ROUNDS[0], a : a + 1, :].rearrange("(p j) o k -> p j (o k)", j=nj),
             )
 
         w2raw = {}
@@ -116,19 +119,17 @@ def tile_psicritic_pa_t_kernel(tc, h1, W2, b2, W3, b3, g1, V2, c2, V3, c3, out):
 
         load_g(0, 2)
         load_w2(3)
-        nc.scalar.dma_start(out=bz[:, 16:20], in_=c2.rearrange("(p t) -> p t", t=4))
-        nc.scalar.dma_start(out=bz[:, 0:12].rearrange("p (a t) -> p a t", a=A), in_=b2.rearrange("a (p t) -> p a t", t=4))
-        nc.scalar.dma_start(out=zrow[0:1, 0 : A * S], in_=b3.rearrange("(o a) s -> o (a s)", o=1))
-        nc.scalar.dma_start(out=zrow[0:1, A * S :], in_=c3.rearrange("(o s) -> o s", o=1))
-        load_h(0, False)
-        load_h_part(0, 0)
+        nc.gpsimd.dma_start(out=bz[:, 16:20], in_=c2.rearrange("(p t) -> p t", t=4))
+        nc.gpsimd.dma_start(out=bz[:, 0:12].rearrange("p (a t) -> p a t", a=A), in_=b2.rearrange("a (p t) -> p a t", t=4))
+        nc.gpsimd.dma_start(out=zrow[0:1, 0 : A * S], in_=b3.rearrange("(o a) s -> o (a s)", o=1))
+        nc.gpsimd.dma_start(out=zrow[0:1, A * S :], in_=c3.rearrange("(o s) -> o s", o=1))
+        load_h_first(0)
         load_w2(0)
-        load_h_part(0, 1)
+        load_h_first(1)
         load_w2(1)
-        load_h_part(0, 2)
-        load_g(1)
+        load_h_first(2)
         load_w2(2)
-        load_h(1, True)
+        load_g(1)
         w3raw = const.tile([P, NS * 4 * S], BF16, name="w3raw")
         nc.sync.dma_start(
             out=w3raw[:, 0 : A * 4 * S].rearrange("p (a x) -> p a x", a=A),
@@ -138,8 +139,9 @@ def tile_psicritic_pa_t_kernel(tc, h1, W2, b2, W3, b3, g1, V2, c2, V3, c3, out):
             out=w3raw[:, A * 4 * S :],
             in_=V3.rearrange("(p t) n -> p (t n)", t=4),
         )
+        load_h(1)
         load_g(2)
-        load_h(2, True)
+        load_h(2)
 
         xt = {}
         xq = {}
@@ -159,17 +161,18 @@ def tile_psicritic_pa_t_kernel(tc, h1, W2, b2, W3, b3, g1, V2, c2, V3, c3, out):
             return (chunks(u // NS) + 1) // 2
 
         def b_on_vector(u, hf):
-            return hf == 1 and u % V_COPIES == 2
+            return hf == 1 and (u == 0 or u % V_COPIES == V_COPIES - 2)
 
         def st_a(u, hf):
             r, s = unit(u)
             nj = min(2, chunks(r) - 2 * hf)
-            x32 = (xg[r] if s == 3 else xh[r])[:].bitcast(F32)
+            own = s == 3 or r == 0
+            x32 = (xg[r] if s == 3 else h_first[s] if r == 0 else xh[r])[:].bitcast(F32)
             xt[u, hf] = ps_x.tile([P, 512], F32, name="xt", tag="xt")
             for uu in range(2):
                 for jj in range(nj):
                     j = 2 * hf + jj
-                    col = j * 256 if s == 3 else (j * A + s) * 256
+                    col = j * 256 if own else (j * A + s) * 256
                     nc.tensor.transpose(
                         xt[u, hf][:, (nj * uu + jj) * P : (nj * uu + jj + 1) * P],
                         x32[:, col + uu : col + 256 : 2],
@@ -289,44 +292,54 @@ def tile_psicritic_pa_t_kernel(tc, h1, W2, b2, W3, b3, g1, V2, c2, V3, c3, out):
                 op0=ALU.mult,
                 op1=ALU.add,
             )
-            if j == nj - 1:
-                rows = out[base[r] : base[r] + ROUNDS[r]]
+            rows = out[base[r] : base[r] + ROUNDS[r]]
+            if r == NR - 1:
+                nc.sync.dma_start(
+                    out=rows.rearrange("(p j) a s -> p j (a s)", j=nj)[:, j : j + 1, :],
+                    in_=osb[r][:, A * S * j : A * S * (j + 1)].unsqueeze(1),
+                )
+            elif j == nj - 1:
                 nc.sync.dma_start(out=rows.rearrange("(p j) a s -> p (j a s)", j=nj), in_=osb[r][:])
 
         def setup_beta():
             pb = ps_o.tile([P, 4 * S], F32, name="pb", tag="ops")
-            nc.tensor.matmul(out=pb[:], lhsT=ones[:], rhs=zrow[:], start=True, stop=True)
-            bb = const.tile([P, 4 * S], F32, name="bb")
-            nc.vector.tensor_copy(out=bb[:], in_=pb[:])
-            m1 = const.tile([P, S], F32, name="m1")
-            nc.vector.tensor_tensor(out=m1[:], in0=bb[:, 0:S], in1=bb[:, S : 2 * S], op=ALU.add)
-            m2 = const.tile([P, S], F32, name="m2")
-            nc.vector.tensor_tensor(out=m2[:], in0=m1[:], in1=bb[:, 2 * S : 3 * S], op=ALU.add)
-            gm = const.tile([P, S], F32, name="gm")
-            nc.vector.scalar_tensor_tensor(
-                out=gm[:], in0=m2[:], scalar=-1.0 / 3.0, in1=bb[:, 3 * S :], op0=ALU.mult, op1=ALU.add
-            )
-            nc.vector.tensor_tensor(
-                out=beta[:].rearrange("p (a s) -> p a s", a=A),
-                in0=bb[:, 0 : A * S].rearrange("p (a s) -> p a s", a=A),
-                in1=gm[:].unsqueeze(1).to_broadcast([P, A, S]),
-                op=ALU.add,
+            dst = pb[:, 0 : A * S]
+            nc.tensor.matmul(out=dst, lhsT=threes[:], rhs=zrow[:, 0 : A * S], start=True, stop=False)
+            for b in range(A + 1):
+                nc.tensor.matmul(
+                    out=dst,
+                    lhsT=(minus if b < A else threes)[:],
+                    rhs=zrow[:, S * b : S * (b + 1)].unsqueeze(1).to_broadcast([P, A, S]),
+                    start=False,
+                    stop=b == A,
+                )
+            nc.vector.tensor_scalar(
+                out=beta[:], in0=dst, scalar1=1.0 / 3.0, scalar2=0.0, op0=ALU.mult, op1=ALU.add
             )
 
-        def setup_w3():
-            w3g = const.tile([P, 8 * 4 * S], BF16, name="w3g", align_bytes=64)
-            for lo, hi, src_lo, factor in ((0, 4, 0, 2.0), (4, 7, 0, -1.0), (7, 8, 3, 1.0)):
-                nc.gpsimd.tensor_scalar(
-                    out=w3g[:, 4 * S * lo : 4 * S * hi].rearrange("p (s n t) -> p s n t", s=hi - lo, t=4),
-                    in0=w3raw[:, 4 * S * src_lo : 4 * S * (src_lo + hi - lo)].rearrange(
-                        "p (s t n) -> p s n t", s=hi - lo, t=4
-                    ),
+        w3g = const.tile([P, 8 * 4 * S], BF16, name="w3g", align_bytes=64)
+
+        def prep_w3_first():
+            for s in range(NS):
+                nc.vector.tensor_scalar(
+                    out=w3g[:, 4 * S * s : 4 * S * (s + 1)].rearrange("p (c i t) -> p c t i", i=4, t=4),
+                    in0=w3raw[:, 4 * S * s : 4 * S * (s + 1)].rearrange("p (t c i) -> p c t i", t=4, i=4),
+                    scalar1=2.0,
+                    scalar2=0.0,
+                    op0=ALU.mult,
+                    op1=ALU.add,
+                )
+
+        def prep_w3_rest():
+            for lo, hi, src_lo, factor in ((4, 7, 0, -0.5), (7, 8, 3, 0.5)):
+                nc.vector.tensor_scalar(
+                    out=w3g[:, 4 * S * lo : 4 * S * hi],
+                    in0=w3g[:, 4 * S * src_lo : 4 * S * (src_lo + hi - lo)],
                     scalar1=factor,
                     scalar2=0.0,
                     op0=ALU.mult,
                     op1=ALU.add,
                 )
-            return w3g
 
         ready = []
         h_done = []
@@ -362,57 +375,63 @@ def tile_psicritic_pa_t_kernel(tc, h1, W2, b2, W3, b3, g1, V2, c2, V3, c3, out):
 
         ctx.enter_context(pinned)
         both_a(0)
-        wg3 = prep_w2(3)
         both_b(0, False)
+        both_b(0, True)
+        wg3 = prep_w2(3)
         both_a(1)
-        quant_w2(3, wg3)
+        both_b(1, False)
         st_c(0)
+        quant_w2(3, wg3)
         for t in range(4):
             st_d(0, t)
-        both_b(1, False)
-        both_a(2)
-        wg0 = prep_w2(0)
-        st_c(1)
-        quant_w2(0, wg0)
-        both_b(2, False)
-        both_b(2, True)
-        later = {0: prep_w2(1), 1: None, 2: None}
-        w3g = setup_w3()
+        wg = {0: prep_w2(0)}
+        state.update(a=2, b=2, c=1)
         for n in range(NU + 1):
-            if n + 3 < NU:
-                both_a(n + 3)
+            lead = 2 if n < 3 else 3
+            first_b = state["b"]
+            while state["a"] < min(NU, n + lead + 1):
+                both_a(state["a"])
+                state["a"] += 1
             if n % NS == 0 and n // NS + 3 < NR:
                 load_g(n // NS + 3)
-                load_h(n // NS + 3, True)
+                load_h(n // NS + 3)
+            if n >= 4:
+                st_f(n - 1)
+            while state["c"] < first_b:
+                st_c(state["c"])
+                state["c"] += 1
+            if n < 3:
+                quant_w2(n, wg[n])
+                if n < 2:
+                    wg[n + 1] = prep_w2(n + 1)
+            if n == 4:
+                prep_w3_rest()
             try_h(n)
             for t in range(4):
                 if n < NU:
                     st_e(n, t)
                 if n + 1 < NU:
                     st_d(n + 1, t)
-            if n + 3 < NU:
-                both_b(n + 3, False)
+            for u in range(first_b, state["a"]):
+                both_b(u, False)
+            state["b"] = state["a"]
             chunk = pop_i(n)
-            if n >= 1:
+            if 1 <= n < 4:
                 st_f(n - 1)
-            if n + 2 < NU:
-                st_c(n + 2)
-            if n < 2:
-                quant_w2(n + 1, later[n])
-            if n == 0:
-                later[1] = prep_w2(2)
+            if n == 4:
+                nc.vector.quantize_mx(out=w3c[:].bitcast(FP8X4), scales=w3s[:], in_=w3g[:])
             if n == 2:
                 setup_beta()
+            if n == 3:
+                prep_w3_first()
             if chunk:
                 st_i1(chunk[0], chunk[1])
             if n >= 1:
                 quantise_h(n - 1, n)
             if chunk:
                 st_i2(chunk[0], chunk[1])
-            if n + 3 < NU:
-                both_b(n + 3, True)
-            if n == 4:
-                nc.vector.quantize_mx(out=w3c[:].bitcast(FP8X4), scales=w3s[:], in_=w3g[:])
+            for u in range(first_b, state["b"]):
+                both_b(u, True)
         n = NU + 1
         while state["i"] < B // P:
             try_h(n)

@@ -119,10 +119,8 @@ def tile_psicritic_pa_t_kernel(tc, h1, W2, b2, W3, b3, g1, V2, c2, V3, c3, out):
 
         load_g(0, 2)
         load_w2(3)
-        nc.gpsimd.dma_start(out=bz[:, 16:20], in_=c2.rearrange("(p t) -> p t", t=4))
-        nc.gpsimd.dma_start(out=bz[:, 0:12].rearrange("p (a t) -> p a t", a=A), in_=b2.rearrange("a (p t) -> p a t", t=4))
-        nc.gpsimd.dma_start(out=zrow[0:1, 0 : A * S], in_=b3.rearrange("(o a) s -> o (a s)", o=1))
-        nc.gpsimd.dma_start(out=zrow[0:1, A * S :], in_=c3.rearrange("(o s) -> o s", o=1))
+        nc.scalar.dma_start(out=bz[:, 16:20], in_=c2.rearrange("(p t) -> p t", t=4))
+        nc.scalar.dma_start(out=bz[:, 0:12].rearrange("p (a t) -> p a t", a=A), in_=b2.rearrange("a (p t) -> p a t", t=4))
         load_h_first(0)
         load_w2(0)
         load_h_first(1)
@@ -130,6 +128,8 @@ def tile_psicritic_pa_t_kernel(tc, h1, W2, b2, W3, b3, g1, V2, c2, V3, c3, out):
         load_h_first(2)
         load_w2(2)
         load_g(1)
+        nc.sync.dma_start(out=zrow[0:1, 0 : A * S], in_=b3.rearrange("(o a) s -> o (a s)", o=1))
+        nc.sync.dma_start(out=zrow[0:1, A * S :], in_=c3.rearrange("(o s) -> o s", o=1))
         w3raw = const.tile([P, NS * 4 * S], BF16, name="w3raw")
         nc.sync.dma_start(
             out=w3raw[:, 0 : A * 4 * S].rearrange("p (a x) -> p a x", a=A),
@@ -260,11 +260,13 @@ def tile_psicritic_pa_t_kernel(tc, h1, W2, b2, W3, b3, g1, V2, c2, V3, c3, out):
                     for b in range(A):
                         l2_pass(dst, r, b, j, b if b == a else 4 + b, False, b == A - 1)
                 else:
-                    l2_pass(dst, r, 3, j, 3, True, False)
-                    l2_pass(dst, r, a, j, a, False, True)
+                    l2_pass(dst, r, a, j, a, True, True)
             if not is_full(r, j):
+                dst = ops[r, j][:, S * A :]
+                l2_pass(dst, r, 3, j, 3, True, False)
+                l2_pass(dst, r, 3, j, 7, False, False)
                 for a in range(A):
-                    l2_pass(ops[r, j][:, S * A :], r, a, j, 4 + a, a == 0, a == A - 1)
+                    l2_pass(dst, r, a, j, 4 + a, False, a == A - 1)
 
         def st_i1(r, j):
             if is_full(r, j):

@@ -14,19 +14,22 @@ ALU = mybir.AluOpType
 P = 128
 B, A, S, F = 4096, 3, 128, 512
 NS = A + 1
+NR = 8
+RT = B // NR
+NJ = RT // P
 ORDER = (3, 0, 1, 2)
-ROUNDS = (512, 512, 512, 512, 512, 512, 512, 256, 256)
-NR = len(ROUNDS)
-NU = NR * NS
+FIRST = [(0, 3, 0, 2), (0, 3, 2, 2), (0, 0, 0, 4), (0, 1, 0, 4), (0, 2, 0, 4)]
+LAST = [(7, 3, 0, 4), (7, 0, 0, 4), (7, 1, 0, 2), (7, 2, 0, 2), (7, 1, 2, 2), (7, 2, 2, 1), (7, 2, 3, 1)]
+UNITS = FIRST + [(r, s, 0, 4) for r in range(1, 7) for s in ORDER] + LAST
+NU = len(UNITS)
 FLOPS = 2 * NS * B * (F * F + F * S)
 
-V_COPIES = 8
+V_COPIES = 3
 ENGINES = {mybir.EngineType.PE, mybir.EngineType.Activation, mybir.EngineType.DVE}
 
 
 def tile_psicritic_pa_t_kernel(tc, h1, W2, b2, W3, b3, g1, V2, c2, V3, c3, out):
     nc = tc.nc
-    base = [sum(ROUNDS[:r]) for r in range(NR)]
     with ExitStack() as ctx:
         const = ctx.enter_context(tc.tile_pool(name="const", bufs=1))
         wst = ctx.enter_context(tc.tile_pool(name="wst", bufs=2))
@@ -61,17 +64,13 @@ def tile_psicritic_pa_t_kernel(tc, h1, W2, b2, W3, b3, g1, V2, c2, V3, c3, out):
         xh = {}
         xg = {}
 
-        def chunks(r):
-            return ROUNDS[r] // P
-
         def is_full(r, j):
-            return r == NR - 1 or (ROUNDS[r] == 512 and j % 2 == 0)
+            return j % 2 == 0
 
         def load_g(r, parts=1):
-            nj = chunks(r)
-            xg[r] = xin.tile([P, nj * F], BF16, name="xg", tag="xg")
-            rows = g1[base[r] : base[r] + ROUNDS[r], :].rearrange("(p j) k -> p j k", j=nj)
-            step = nj // parts
+            xg[r] = xin.tile([P, NJ * F], BF16, name="xg", tag="xg")
+            rows = g1[RT * r : RT * (r + 1), :].rearrange("(p j) k -> p j k", j=NJ)
+            step = NJ // parts
             for i in range(parts):
                 nc.sync.dma_start(
                     out=xg[r][:, F * step * i : F * step * (i + 1)].rearrange("p (j k) -> p j k", k=F),
@@ -79,19 +78,17 @@ def tile_psicritic_pa_t_kernel(tc, h1, W2, b2, W3, b3, g1, V2, c2, V3, c3, out):
                 )
 
         def load_h(r):
-            nj = chunks(r)
-            xh[r] = xin.tile([P, nj * A * F], BF16, name="xh", tag="xh")
-            rows = h1[base[r] : base[r] + ROUNDS[r]]
-            nc.sync.dma_start(out=xh[r][:], in_=rows.rearrange("(p j) a k -> p (j a k)", j=nj))
+            xh[r] = xin.tile([P, NJ * A * F], BF16, name="xh", tag="xh")
+            rows = h1[RT * r : RT * (r + 1)]
+            nc.sync.dma_start(out=xh[r][:], in_=rows.rearrange("(p j) a k -> p (j a k)", j=NJ))
 
         h_first = {}
 
         def load_h_first(a):
-            nj = chunks(0)
-            h_first[a] = const.tile([P, nj * F], BF16, name="h_first%d" % a)
+            h_first[a] = const.tile([P, NJ * F], BF16, name="h_first%d" % a)
             nc.sync.dma_start(
-                out=h_first[a][:].rearrange("p (j k) -> p j k", j=nj),
-                in_=h1[0 : ROUNDS[0], a : a + 1, :].rearrange("(p j) o k -> p j (o k)", j=nj),
+                out=h_first[a][:].rearrange("p (j k) -> p j k", j=NJ),
+                in_=h1[0:RT, a : a + 1, :].rearrange("(p j) o k -> p j (o k)", j=NJ),
             )
 
         w2raw = {}
@@ -117,8 +114,8 @@ def tile_psicritic_pa_t_kernel(tc, h1, W2, b2, W3, b3, g1, V2, c2, V3, c3, out):
                 in_=wg[:],
             )
 
-        load_g(0, 2)
         load_w2(3)
+        load_g(0, 4)
         nc.scalar.dma_start(out=bz[:, 16:20], in_=c2.rearrange("(p t) -> p t", t=4))
         nc.scalar.dma_start(out=bz[:, 0:12].rearrange("p (a t) -> p a t", a=A), in_=b2.rearrange("a (p t) -> p a t", t=4))
         load_h_first(0)
@@ -142,6 +139,7 @@ def tile_psicritic_pa_t_kernel(tc, h1, W2, b2, W3, b3, g1, V2, c2, V3, c3, out):
         load_h(1)
         load_g(2)
         load_h(2)
+        load_h(3)
 
         xt = {}
         xq = {}
@@ -154,24 +152,24 @@ def tile_psicritic_pa_t_kernel(tc, h1, W2, b2, W3, b3, g1, V2, c2, V3, c3, out):
         osb = {}
         esb = {}
 
-        def unit(u):
-            return u // NS, ORDER[u % NS]
+        def tokens(u):
+            return P * UNITS[u][3]
 
         def halves(u):
-            return (chunks(u // NS) + 1) // 2
+            return (UNITS[u][3] + 1) // 2
 
         def b_on_vector(u, hf):
-            return hf == 1 and (u == 0 or u % V_COPIES == V_COPIES - 2)
+            return hf == 1 and u % V_COPIES == 0 and 6 < u < NU - 11
 
         def st_a(u, hf):
-            r, s = unit(u)
-            nj = min(2, chunks(r) - 2 * hf)
+            r, s, j0, nj = UNITS[u]
+            nj = min(2, nj - 2 * hf)
             own = s == 3 or r == 0
             x32 = (xg[r] if s == 3 else h_first[s] if r == 0 else xh[r])[:].bitcast(F32)
             xt[u, hf] = ps_x.tile([P, 512], F32, name="xt", tag="xt")
             for uu in range(2):
                 for jj in range(nj):
-                    j = 2 * hf + jj
+                    j = j0 + 2 * hf + jj
                     col = j * 256 if own else (j * A + s) * 256
                     nc.tensor.transpose(
                         xt[u, hf][:, (nj * uu + jj) * P : (nj * uu + jj + 1) * P],
@@ -180,10 +178,9 @@ def tile_psicritic_pa_t_kernel(tc, h1, W2, b2, W3, b3, g1, V2, c2, V3, c3, out):
                     )
 
         def st_b(u, hf):
-            r, s = unit(u)
-            nj = min(2, chunks(r) - 2 * hf)
+            nj = min(2, UNITS[u][3] - 2 * hf)
             if hf == 0:
-                xq[u] = xqp.tile([P, 4 * ROUNDS[r]], BF16, name="xq", tag="xq", align_bytes=64)
+                xq[u] = xqp.tile([P, 4 * tokens(u)], BF16, name="xq", tag="xq", align_bytes=64)
             dst = xq[u][:].bitcast(F32).rearrange("p (w u) -> p w u", u=2)[:, 256 * hf : 256 * hf + P * nj, :]
             src = xt[u, hf][:, 0 : 2 * P * nj].rearrange("p (u w) -> p w u", u=2)
             if b_on_vector(u, hf):
@@ -192,18 +189,17 @@ def tile_psicritic_pa_t_kernel(tc, h1, W2, b2, W3, b3, g1, V2, c2, V3, c3, out):
                 nc.scalar.copy(out=dst, in_=src)
 
         def st_c(u):
-            n_tok = ROUNDS[u // NS]
-            codes = xqp.tile([P, n_tok], U32, name="xc", tag="xc", align_bytes=64)
-            scales = xqp.tile([P, n_tok], U8, name="xs", tag="xs", align_bytes=64)
+            codes = xqp.tile([P, tokens(u)], U32, name="xc", tag="xc", align_bytes=64)
+            scales = xqp.tile([P, tokens(u)], U8, name="xs", tag="xs", align_bytes=64)
             xc[u] = (codes, scales)
             nc.vector.quantize_mx(out=codes[:].bitcast(FP8X4), scales=scales[:], in_=xq[u][:])
 
         def st_d(u, t):
-            r, s = unit(u)
+            s = UNITS[u][1]
             hps[u, t] = ps_h.tile([P, 512], F32, name="hps", tag="hps")
             col = F * s + P * t
             nc.tensor.matmul_mx(
-                out=hps[u, t][:, 0 : ROUNDS[r]],
+                out=hps[u, t][:, 0 : tokens(u)],
                 lhsT=w2c[:, col : col + P].bitcast(FP8X4),
                 lhsT_scale=w2s[:, col : col + P],
                 rhs=xc[u][0][:].bitcast(FP8X4),
@@ -213,37 +209,38 @@ def tile_psicritic_pa_t_kernel(tc, h1, W2, b2, W3, b3, g1, V2, c2, V3, c3, out):
             )
 
         def st_e(u, t):
-            r, s = unit(u)
-            n_tok = ROUNDS[r]
+            s, n_tok = UNITS[u][1], tokens(u)
             if t == 0:
                 hp[u] = hpp.tile([P, 4 * n_tok], BF16, name="hp", tag="hp")
+            col = 4 * (4 if s == 3 else s) + t
             nc.scalar.activation(
                 out=hp[u][:, n_tok * t : n_tok * (t + 1)],
                 in_=hps[u, t][:, 0:n_tok],
                 func=ACT.Relu,
-                bias=bz[:, 4 * (4 if s == 3 else s) + t : 4 * (4 if s == 3 else s) + t + 1],
+                bias=bz[:, col : col + 1],
                 scale=1.0,
             )
 
         def st_f(u):
-            hq[u] = hpp.tile([P, 4 * ROUNDS[u // NS]], BF16, name="hq", tag="hq", align_bytes=64)
+            hq[u] = hpp.tile([P, 4 * tokens(u)], BF16, name="hq", tag="hq", align_bytes=64)
             nc.vector.tensor_copy(
                 out=hq[u][:].rearrange("p (c i t) -> p c t i", i=4, t=4),
                 in_=hp[u][:].rearrange("p (t c i) -> p c t i", t=4, i=4),
             )
 
         def st_g(u):
-            r, s = unit(u)
-            codes = hcp.tile([P, ROUNDS[r]], U32, name="hc%d" % s, tag="hc%d" % s, align_bytes=64)
-            scales = hcp.tile([P, ROUNDS[r]], U8, name="hs%d" % s, tag="hs%d" % s, align_bytes=64)
-            hc[r, s] = (codes, scales)
+            r, s, j0, nj = UNITS[u]
+            codes = hcp.tile([P, tokens(u)], U32, name="hc%d" % s, tag="hc%d" % s, align_bytes=64)
+            scales = hcp.tile([P, tokens(u)], U8, name="hs%d" % s, tag="hs%d" % s, align_bytes=64)
+            for j in range(nj):
+                hc[r, s, j0 + j] = (codes[:, P * j : P * (j + 1)], scales[:, P * j : P * (j + 1)])
             nc.vector.quantize_mx(out=codes[:].bitcast(FP8X4), scales=scales[:], in_=hq[u][:])
 
         def l2_pass(dst, r, s, j, blk, start, stop):
             nc.tensor.matmul_mx(
                 out=dst,
-                lhsT=hc[r, s][0][:, P * j : P * (j + 1)].bitcast(FP8X4),
-                lhsT_scale=hc[r, s][1][:, P * j : P * (j + 1)],
+                lhsT=hc[r, s, j][0].bitcast(FP8X4),
+                lhsT_scale=hc[r, s, j][1],
                 rhs=w3c[:, S * blk : S * (blk + 1)].bitcast(FP8X4),
                 rhs_scale=w3s[:, S * blk : S * (blk + 1)],
                 start=start,
@@ -268,6 +265,26 @@ def tile_psicritic_pa_t_kernel(tc, h1, W2, b2, W3, b3, g1, V2, c2, V3, c3, out):
                 for a in range(A):
                     l2_pass(dst, r, a, j, 4 + a, False, a == A - 1)
 
+        end_bank = {}
+
+        def st_h_open():
+            r, j = NR - 1, NJ - 1
+            for a in range(A):
+                if a == 2:
+                    end_bank[a] = ps_o.tile([P, 4 * S], F32, name="end", tag="ops")
+                else:
+                    end_bank[a] = ps_x.tile([P, 512], F32, name="end", tag="xt")
+                dst = end_bank[a][:, 0:S]
+                l2_pass(dst, r, 3, j, 3, True, False)
+                l2_pass(dst, r, 3, j, 7, False, False)
+                for b in range(A - 1):
+                    l2_pass(dst, r, b, j, b if b == a else 4 + b, False, False)
+
+        def st_h_close():
+            r, j, b = NR - 1, NJ - 1, A - 1
+            for a in range(A):
+                l2_pass(end_bank[a][:, 0:S], r, b, j, b if b == a else 4 + b, False, True)
+
         def st_i1(r, j):
             if is_full(r, j):
                 return
@@ -281,10 +298,12 @@ def tile_psicritic_pa_t_kernel(tc, h1, W2, b2, W3, b3, g1, V2, c2, V3, c3, out):
                 op1=ALU.add,
             )
 
+        def out_rows(r):
+            return out[RT * r : RT * (r + 1)].rearrange("(p j) a s -> p j (a s)", j=NJ)
+
         def st_i2(r, j):
-            nj = chunks(r)
             if j == 0:
-                osb[r] = outp.tile([P, nj * A * S], F32, name="osb", tag="osb")
+                osb[r] = outp.tile([P, NJ * A * S], F32, name="osb", tag="osb")
             full = is_full(r, j)
             nc.vector.scalar_tensor_tensor(
                 out=osb[r][:, A * S * j : A * S * (j + 1)],
@@ -294,14 +313,29 @@ def tile_psicritic_pa_t_kernel(tc, h1, W2, b2, W3, b3, g1, V2, c2, V3, c3, out):
                 op0=ALU.mult,
                 op1=ALU.add,
             )
-            rows = out[base[r] : base[r] + ROUNDS[r]]
             if r == NR - 1:
-                nc.sync.dma_start(
-                    out=rows.rearrange("(p j) a s -> p j (a s)", j=nj)[:, j : j + 1, :],
-                    in_=osb[r][:, A * S * j : A * S * (j + 1)].unsqueeze(1),
+                store(r, j, 1)
+            elif j == NJ - 1:
+                store(r, 0, NJ)
+
+        def store(r, j, n):
+            nc.sync.dma_start(
+                out=out_rows(r)[:, j : j + n, :],
+                in_=osb[r][:, A * S * j : A * S * (j + n)].rearrange("p (j x) -> p j x", j=n),
+            )
+
+        def st_i_end():
+            r, j = NR - 1, NJ - 1
+            for a in range(A):
+                nc.vector.scalar_tensor_tensor(
+                    out=osb[r][:, A * S * j + S * a : A * S * j + S * (a + 1)],
+                    in0=end_bank[a][:, 0:S],
+                    scalar=1.0 / 3.0,
+                    in1=beta[:, S * a : S * (a + 1)],
+                    op0=ALU.mult,
+                    op1=ALU.add,
                 )
-            elif j == nj - 1:
-                nc.sync.dma_start(out=rows.rearrange("(p j) a s -> p (j a s)", j=nj), in_=osb[r][:])
+            store(r, j, 1)
 
         def setup_beta():
             pb = ps_o.tile([P, 4 * S], F32, name="pb", tag="ops")
@@ -345,13 +379,16 @@ def tile_psicritic_pa_t_kernel(tc, h1, W2, b2, W3, b3, g1, V2, c2, V3, c3, out):
 
         ready = []
         h_done = []
-        state = {"h": 0, "i": 0}
+        state = {"a": 2, "b": 2, "c": 2, "h": 0, "i": 0}
+        count = {}
 
         def quantise_h(u, n):
             st_g(u)
-            if u % NS == NS - 1:
-                for j in range(chunks(u // NS)):
-                    ready.append((u // NS, j, n))
+            r, s, j0, nj = UNITS[u]
+            for j in range(j0, j0 + nj):
+                count[r, j] = count.get((r, j), 0) + 1
+                if count[r, j] == NS and (r, j) != (NR - 1, NJ - 1):
+                    ready.append((r, j, n))
 
         def try_h(n):
             if state["h"] < len(ready) and ready[state["h"]][2] <= n - 1:
@@ -369,6 +406,11 @@ def tile_psicritic_pa_t_kernel(tc, h1, W2, b2, W3, b3, g1, V2, c2, V3, c3, out):
         def both_a(u):
             for hf in range(halves(u)):
                 st_a(u, hf)
+            r = UNITS[u][0]
+            if u + 1 < NU and UNITS[u + 1][0] > r and r + 3 < NR:
+                load_g(r + 3)
+                if r + 3 > 3:
+                    load_h(r + 3)
 
         def both_b(u, vector):
             for hf in range(halves(u)):
@@ -377,27 +419,23 @@ def tile_psicritic_pa_t_kernel(tc, h1, W2, b2, W3, b3, g1, V2, c2, V3, c3, out):
 
         ctx.enter_context(pinned)
         both_a(0)
-        both_b(0, False)
-        both_b(0, True)
-        wg3 = prep_w2(3)
         both_a(1)
+        wg3 = prep_w2(3)
+        both_b(0, False)
         both_b(1, False)
-        st_c(0)
         quant_w2(3, wg3)
+        st_c(0)
         for t in range(4):
             st_d(0, t)
+        st_c(1)
         wg = {0: prep_w2(0)}
-        state.update(a=2, b=2, c=1)
         for n in range(NU + 1):
-            lead = 2 if n < 3 else 3
+            lead = 2 if n < 4 else 3
             first_b = state["b"]
             while state["a"] < min(NU, n + lead + 1):
                 both_a(state["a"])
                 state["a"] += 1
-            if n % NS == 0 and n // NS + 3 < NR:
-                load_g(n // NS + 3)
-                load_h(n // NS + 3)
-            if n >= 4:
+            if n >= 5:
                 st_f(n - 1)
             while state["c"] < first_b:
                 st_c(state["c"])
@@ -406,8 +444,10 @@ def tile_psicritic_pa_t_kernel(tc, h1, W2, b2, W3, b3, g1, V2, c2, V3, c3, out):
                 quant_w2(n, wg[n])
                 if n < 2:
                     wg[n + 1] = prep_w2(n + 1)
-            if n == 4:
+            if n == 5:
                 prep_w3_rest()
+            if n == NU - 1:
+                st_h_open()
             try_h(n)
             for t in range(4):
                 if n < NU:
@@ -418,13 +458,13 @@ def tile_psicritic_pa_t_kernel(tc, h1, W2, b2, W3, b3, g1, V2, c2, V3, c3, out):
                 both_b(u, False)
             state["b"] = state["a"]
             chunk = pop_i(n)
-            if 1 <= n < 4:
+            if 1 <= n < 5:
                 st_f(n - 1)
-            if n == 4:
+            if n == 5:
                 nc.vector.quantize_mx(out=w3c[:].bitcast(FP8X4), scales=w3s[:], in_=w3g[:])
-            if n == 2:
-                setup_beta()
             if n == 3:
+                setup_beta()
+            if n == 4:
                 prep_w3_first()
             if chunk:
                 st_i1(chunk[0], chunk[1])
@@ -434,11 +474,13 @@ def tile_psicritic_pa_t_kernel(tc, h1, W2, b2, W3, b3, g1, V2, c2, V3, c3, out):
                 st_i2(chunk[0], chunk[1])
             for u in range(first_b, state["b"]):
                 both_b(u, True)
+        st_h_close()
         n = NU + 1
-        while state["i"] < B // P:
+        while state["i"] < B // P - 1:
             try_h(n)
             chunk = pop_i(n)
             if chunk:
                 st_i1(chunk[0], chunk[1])
                 st_i2(chunk[0], chunk[1])
             n += 1
+        st_i_end()

@@ -24,7 +24,7 @@ UNITS = FIRST + [(r, s, 0, 4) for r in range(1, 7) for s in ORDER] + LAST
 NU = len(UNITS)
 FLOPS = 2 * NS * B * (F * F + F * S)
 
-V_COPIES = 3
+V_COPIES = 400
 ENGINES = {mybir.EngineType.PE, mybir.EngineType.Activation, mybir.EngineType.DVE}
 
 
@@ -52,20 +52,21 @@ def tile_psicritic_pa_t_kernel(tc, h1, W2, b2, W3, b3, g1, V2, c2, V3, c3, out):
         warm = const.tile([P, 16], BF16, name="warm")
         nc.scalar.activation(out=warm[:, 0:1], in_=threes[:, 0:1], func=ACT.Relu)
         bz = const.tile([P, 32], BF16, name="bz")
+        bias2 = const.tile([P, 32], F32, name="bias2")
         zrow = const.tile([P, 4 * S], BF16, name="zrow")
         nc.vector.memset(zrow[:], 0.0)
 
-        w2c = const.tile([P, NS * F], U32, name="w2c", align_bytes=64)
-        w2s = const.tile([P, NS * F], U8, name="w2s", align_bytes=64)
-        w3c = const.tile([P, 8 * S], U32, name="w3c", align_bytes=64)
-        w3s = const.tile([P, 8 * S], U8, name="w3s", align_bytes=64)
+        w2c = const.tile([P, NS * F], U32, name="w2c", align_bytes=256)
+        w2s = const.tile([P, NS * F], U8, name="w2s", align_bytes=256)
+        w3c = const.tile([P, 8 * S], U32, name="w3c", align_bytes=256)
+        w3s = const.tile([P, 8 * S], U8, name="w3s", align_bytes=256)
         beta = const.tile([P, A * S], F32, name="beta")
 
         xh = {}
         xg = {}
 
         def is_full(r, j):
-            return j % 2 == 0
+            return j % 2 == 0 or (j == 3 and r % 2 == 0)
 
         def load_g(r, parts=1):
             xg[r] = xin.tile([P, NJ * F], BF16, name="xg", tag="xg")
@@ -101,7 +102,7 @@ def tile_psicritic_pa_t_kernel(tc, h1, W2, b2, W3, b3, g1, V2, c2, V3, c3, out):
             nc.sync.dma_start(out=w2raw[s][:], in_=src)
 
         def prep_w2(s):
-            wg = wst.tile([P, 4 * F], BF16, name="wg", tag="wg", align_bytes=64)
+            wg = wst.tile([P, 4 * F], BF16, name="wg", tag="wg", align_bytes=256)
             dst = wg[:].rearrange("p (t m j) -> p t m j", t=4, j=4)
             src = w2raw[s][:].rearrange("p (j m t) -> p t m j", t=4, j=4)
             nc.vector.tensor_copy(out=dst, in_=src)
@@ -180,7 +181,7 @@ def tile_psicritic_pa_t_kernel(tc, h1, W2, b2, W3, b3, g1, V2, c2, V3, c3, out):
         def st_b(u, hf):
             nj = min(2, UNITS[u][3] - 2 * hf)
             if hf == 0:
-                xq[u] = xqp.tile([P, 4 * tokens(u)], BF16, name="xq", tag="xq", align_bytes=64)
+                xq[u] = xqp.tile([P, 4 * tokens(u)], BF16, name="xq", tag="xq", align_bytes=256)
             dst = xq[u][:].bitcast(F32).rearrange("p (w u) -> p w u", u=2)[:, 256 * hf : 256 * hf + P * nj, :]
             src = xt[u, hf][:, 0 : 2 * P * nj].rearrange("p (u w) -> p w u", u=2)
             if b_on_vector(u, hf):
@@ -189,8 +190,8 @@ def tile_psicritic_pa_t_kernel(tc, h1, W2, b2, W3, b3, g1, V2, c2, V3, c3, out):
                 nc.scalar.copy(out=dst, in_=src)
 
         def st_c(u):
-            codes = xqp.tile([P, tokens(u)], U32, name="xc", tag="xc", align_bytes=64)
-            scales = xqp.tile([P, tokens(u)], U8, name="xs", tag="xs", align_bytes=64)
+            codes = xqp.tile([P, tokens(u)], U32, name="xc", tag="xc", align_bytes=256)
+            scales = xqp.tile([P, tokens(u)], U8, name="xs", tag="xs", align_bytes=256)
             xc[u] = (codes, scales)
             nc.vector.quantize_mx(out=codes[:].bitcast(FP8X4), scales=scales[:], in_=xq[u][:])
 
@@ -213,16 +214,26 @@ def tile_psicritic_pa_t_kernel(tc, h1, W2, b2, W3, b3, g1, V2, c2, V3, c3, out):
             if t == 0:
                 hp[u] = hpp.tile([P, 4 * n_tok], BF16, name="hp", tag="hp")
             col = 4 * (4 if s == 3 else s) + t
+            if t == 3 and u % 4 == 0 and 6 < u < NU - 11:
+                nc.vector.tensor_scalar(
+                    out=hp[u][:, n_tok * t : n_tok * (t + 1)],
+                    in0=hps[u, t][:, 0:n_tok],
+                    scalar1=bias2[:, col : col + 1],
+                    scalar2=0.0,
+                    op0=ALU.add,
+                    op1=ALU.max,
+                )
+                return
             nc.scalar.activation(
                 out=hp[u][:, n_tok * t : n_tok * (t + 1)],
                 in_=hps[u, t][:, 0:n_tok],
                 func=ACT.Relu,
-                bias=bz[:, col : col + 1],
+                bias=bias2[:, col : col + 1],
                 scale=1.0,
             )
 
         def st_f(u):
-            hq[u] = hpp.tile([P, 4 * tokens(u)], BF16, name="hq", tag="hq", align_bytes=64)
+            hq[u] = hpp.tile([P, 4 * tokens(u)], BF16, name="hq", tag="hq", align_bytes=256)
             nc.vector.tensor_copy(
                 out=hq[u][:].rearrange("p (c i t) -> p c t i", i=4, t=4),
                 in_=hp[u][:].rearrange("p (t c i) -> p c t i", t=4, i=4),
@@ -230,8 +241,8 @@ def tile_psicritic_pa_t_kernel(tc, h1, W2, b2, W3, b3, g1, V2, c2, V3, c3, out):
 
         def st_g(u):
             r, s, j0, nj = UNITS[u]
-            codes = hcp.tile([P, tokens(u)], U32, name="hc%d" % s, tag="hc%d" % s, align_bytes=64)
-            scales = hcp.tile([P, tokens(u)], U8, name="hs%d" % s, tag="hs%d" % s, align_bytes=64)
+            codes = hcp.tile([P, tokens(u)], U32, name="hc%d" % s, tag="hc%d" % s, align_bytes=256)
+            scales = hcp.tile([P, tokens(u)], U8, name="hs%d" % s, tag="hs%d" % s, align_bytes=256)
             for j in range(nj):
                 hc[r, s, j0 + j] = (codes[:, P * j : P * (j + 1)], scales[:, P * j : P * (j + 1)])
             nc.vector.quantize_mx(out=codes[:].bitcast(FP8X4), scales=scales[:], in_=hq[u][:])
@@ -353,7 +364,7 @@ def tile_psicritic_pa_t_kernel(tc, h1, W2, b2, W3, b3, g1, V2, c2, V3, c3, out):
                 out=beta[:], in0=dst, scalar1=1.0 / 3.0, scalar2=0.0, op0=ALU.mult, op1=ALU.add
             )
 
-        w3g = const.tile([P, 8 * 4 * S], BF16, name="w3g", align_bytes=64)
+        w3g = const.tile([P, 8 * 4 * S], BF16, name="w3g", align_bytes=256)
 
         def prep_w3_first():
             for s in range(NS):
@@ -421,6 +432,8 @@ def tile_psicritic_pa_t_kernel(tc, h1, W2, b2, W3, b3, g1, V2, c2, V3, c3, out):
         both_a(0)
         both_a(1)
         wg3 = prep_w2(3)
+        nc.vector.tensor_copy(out=bias2[:, 16:20], in_=bz[:, 16:20])
+        nc.vector.tensor_copy(out=bias2[:, 0:12], in_=bz[:, 0:12])
         both_b(0, False)
         both_b(1, False)
         quant_w2(3, wg3)
@@ -448,12 +461,13 @@ def tile_psicritic_pa_t_kernel(tc, h1, W2, b2, W3, b3, g1, V2, c2, V3, c3, out):
                 prep_w3_rest()
             if n == NU - 1:
                 st_h_open()
-            try_h(n)
             for t in range(4):
                 if n < NU:
                     st_e(n, t)
                 if n + 1 < NU:
                     st_d(n + 1, t)
+                if t == (1 if n < NU - 4 else 3):
+                    try_h(n)
             for u in range(first_b, state["a"]):
                 both_b(u, False)
             state["b"] = state["a"]
@@ -462,9 +476,9 @@ def tile_psicritic_pa_t_kernel(tc, h1, W2, b2, W3, b3, g1, V2, c2, V3, c3, out):
                 st_f(n - 1)
             if n == 5:
                 nc.vector.quantize_mx(out=w3c[:].bitcast(FP8X4), scales=w3s[:], in_=w3g[:])
-            if n == 3:
+            if n == 5:
                 setup_beta()
-            if n == 4:
+            if n == 3:
                 prep_w3_first()
             if chunk:
                 st_i1(chunk[0], chunk[1])

from contextlib import ExitStack

import concourse.mybir as mybir
from concourse.masks import make_identity

F32 = mybir.dt.float32
BF16 = mybir.dt.bfloat16
U32 = mybir.dt.uint32
U8 = mybir.dt.uint8
FP8X4 = mybir.dt.float8_e4m3fn_x4
ACT = mybir.ActivationFunctionType
ALU = mybir.AluOpType

P = 128
B, A, S, F = 4096, 3, 128, 512
NS = A + 1
NR = 8
RT = B // NR
NJ = RT // P
ORDER = (3, 0, 1, 2)
FIRST = [(0, 3, 0, 2), (0, 3, 2, 2), (0, 0, 0, 4), (0, 1, 0, 4), (0, 2, 0, 4)]
LAST = [(7, 3, 0, 4), (7, 0, 0, 4), (7, 1, 0, 2), (7, 2, 0, 2), (7, 1, 2, 2), (7, 2, 2, 1), (7, 2, 3, 1)]
UNITS = FIRST + [(r, s, 0, 4) for r in range(1, 7) for s in ORDER] + LAST
NU = len(UNITS)
FLOPS = 2 * NS * B * (F * F + F * S)

V_COPIES = 400
ENGINES = {mybir.EngineType.PE, mybir.EngineType.Activation, mybir.EngineType.DVE}


def tile_psicritic_pa_t_kernel(tc, h1, W2, b2, W3, b3, g1, V2, c2, V3, c3, out):
    nc = tc.nc
    with ExitStack() as ctx:
        const = ctx.enter_context(tc.tile_pool(name="const", bufs=1))
        wst = ctx.enter_context(tc.tile_pool(name="wst", bufs=2))
        xin = ctx.enter_context(tc.tile_pool(name="xin", bufs=3))
        xqp = ctx.enter_context(tc.tile_pool(name="xqp", bufs=4))
        hpp = ctx.enter_context(tc.tile_pool(name="hpp", bufs=3))
        hcp = ctx.enter_context(tc.tile_pool(name="hcp", bufs=3))
        outp = ctx.enter_context(tc.tile_pool(name="outp", bufs=3))
        pinned = tc.manual_schedule(engines=ENGINES)
        ps_x = ctx.enter_context(tc.psum_pool(name="ps_x", bufs=2))
        ps_h = ctx.enter_context(tc.psum_pool(name="ps_h", bufs=4))
        ps_o = ctx.enter_context(tc.psum_pool(name="ps_o", bufs=2))

        ident = const.tile([P, P], F32, name="ident")
        make_identity(nc, ident[:])
        threes = const.tile([P, P], BF16, name="threes")
        nc.vector.memset(threes[:], 3.0)
        minus = const.tile([P, P], BF16, name="minus")
        nc.vector.memset(minus[:], -1.0)
        warm = const.tile([P, 16], BF16, name="warm")
        nc.scalar.activation(out=warm[:, 0:1], in_=threes[:, 0:1], func=ACT.Relu)
        bz = const.tile([P, 32], BF16, name="bz")
        bias2 = const.tile([P, 32], F32, name="bias2")
        zrow = const.tile([P, 4 * S], BF16, name="zrow")
        nc.vector.memset(zrow[:], 0.0)

        w2c = const.tile([P, NS * F], U32, name="w2c", align_bytes=256)
        w2s = const.tile([P, NS * F], U8, name="w2s", align_bytes=256)
        w3c = const.tile([P, 8 * S], U32, name="w3c", align_bytes=256)
        w3s = const.tile([P, 8 * S], U8, name="w3s", align_bytes=256)
        beta = const.tile([P, A * S], F32, name="beta")

        xh = {}
        xg = {}

        def is_full(r, j):
            return j % 2 == 0 or (j == 3 and r % 2 == 0)

        def load_g(r, parts=1):
            xg[r] = xin.tile([P, NJ * F], BF16, name="xg", tag="xg")
            rows = g1[RT * r : RT * (r + 1), :].rearrange("(p j) k -> p j k", j=NJ)
            step = NJ // parts
            for i in range(parts):
                nc.sync.dma_start(
                    out=xg[r][:, F * step * i : F * step * (i + 1)].rearrange("p (j k) -> p j k", k=F),
                    in_=rows[:, step * i : step * (i + 1), :],
                )

        def load_h(r):
            xh[r] = xin.tile([P, NJ * A * F], BF16, name="xh", tag="xh")
            rows = h1[RT * r : RT * (r + 1)]
            nc.sync.dma_start(out=xh[r][:], in_=rows.rearrange("(p j) a k -> p (j a k)", j=NJ))

        h_first = {}

        def load_h_first(a):
            h_first[a] = const.tile([P, NJ * F], BF16, name="h_first%d" % a)
            nc.sync.dma_start(
                out=h_first[a][:].rearrange("p (j k) -> p j k", j=NJ),
                in_=h1[0:RT, a : a + 1, :].rearrange("(p j) o k -> p j (o k)", j=NJ),
            )

        w2raw = {}

        def load_w2(s):
            w2raw[s] = wst.tile([P, 4 * F], BF16, name="w2raw", tag="w2raw", bufs=4)
            src = V2.rearrange("(p j) n -> p (j n)", j=4) if s == 3 else W2[s : s + 1].rearrange(
                "o (p j) n -> p (o j n)", j=4
            )
            nc.sync.dma_start(out=w2raw[s][:], in_=src)

        def prep_w2(s):
            wg = wst.tile([P, 4 * F], BF16, name="wg", tag="wg", align_bytes=256)
            dst = wg[:].rearrange("p (t m j) -> p t m j", t=4, j=4)
            src = w2raw[s][:].rearrange("p (j m t) -> p t m j", t=4, j=4)
            nc.vector.tensor_copy(out=dst, in_=src)
            return wg

        def quant_w2(s, wg):
            nc.vector.quantize_mx(
                out=w2c[:, F * s : F * (s + 1)].bitcast(FP8X4),
                scales=w2s[:, F * s : F * (s + 1)],
                in_=wg[:],
            )

        load_w2(3)
        load_g(0, 4)
        nc.scalar.dma_start(out=bz[:, 16:20], in_=c2.rearrange("(p t) -> p t", t=4))
        nc.scalar.dma_start(out=bz[:, 0:12].rearrange("p (a t) -> p a t", a=A), in_=b2.rearrange("a (p t) -> p a t", t=4))
        load_h_first(0)
        load_w2(0)
        load_h_first(1)
        load_w2(1)
        load_h_first(2)
        load_w2(2)
        load_g(1)
        nc.sync.dma_start(out=zrow[0:1, 0 : A * S], in_=b3.rearrange("(o a) s -> o (a s)", o=1))
        nc.sync.dma_start(out=zrow[0:1, A * S :], in_=c3.rearrange("(o s) -> o s", o=1))
        w3raw = const.tile([P, NS * 4 * S], BF16, name="w3raw")
        nc.sync.dma_start(
            out=w3raw[:, 0 : A * 4 * S].rearrange("p (a x) -> p a x", a=A),
            in_=W3.rearrange("a (p t) n -> p a (t n)", t=4),
        )
        nc.sync.dma_start(
            out=w3raw[:, A * 4 * S :],
            in_=V3.rearrange("(p t) n -> p (t n)", t=4),
        )
        load_h(1)
        load_g(2)
        load_h(2)
        load_h(3)

        xt = {}
        xq = {}
        xc = {}
        hps = {}
        hp = {}
        hq = {}
        hc = {}
        ops = {}
        osb = {}
        esb = {}

        def tokens(u):
            return P * UNITS[u][3]

        def halves(u):
            return (UNITS[u][3] + 1) // 2

        def b_on_vector(u, hf):
            return hf == 1 and u % V_COPIES == 0 and 6 < u < NU - 11

        def st_a(u, hf):
            r, s, j0, nj = UNITS[u]
            nj = min(2, nj - 2 * hf)
            own = s == 3 or r == 0
            x32 = (xg[r] if s == 3 else h_first[s] if r == 0 else xh[r])[:].bitcast(F32)
            xt[u, hf] = ps_x.tile([P, 512], F32, name="xt", tag="xt")
            for uu in range(2):
                for jj in range(nj):
                    j = j0 + 2 * hf + jj
                    col = j * 256 if own else (j * A + s) * 256
                    nc.tensor.transpose(
                        xt[u, hf][:, (nj * uu + jj) * P : (nj * uu + jj + 1) * P],
                        x32[:, col + uu : col + 256 : 2],
                        ident[:],
                    )

        def st_b(u, hf):
            nj = min(2, UNITS[u][3] - 2 * hf)
            if hf == 0:
                xq[u] = xqp.tile([P, 4 * tokens(u)], BF16, name="xq", tag="xq", align_bytes=256)
            dst = xq[u][:].bitcast(F32).rearrange("p (w u) -> p w u", u=2)[:, 256 * hf : 256 * hf + P * nj, :]
            src = xt[u, hf][:, 0 : 2 * P * nj].rearrange("p (u w) -> p w u", u=2)
            if b_on_vector(u, hf):
                nc.vector.tensor_copy(out=dst, in_=src)
            else:
                nc.scalar.copy(out=dst, in_=src)

        def st_c(u):
            codes = xqp.tile([P, tokens(u)], U32, name="xc", tag="xc", align_bytes=256)
            scales = xqp.tile([P, tokens(u)], U8, name="xs", tag="xs", align_bytes=256)
            xc[u] = (codes, scales)
            nc.vector.quantize_mx(out=codes[:].bitcast(FP8X4), scales=scales[:], in_=xq[u][:])

        def st_d(u, t):
            s = UNITS[u][1]
            hps[u, t] = ps_h.tile([P, 512], F32, name="hps", tag="hps")
            col = F * s + P * t
            nc.tensor.matmul_mx(
                out=hps[u, t][:, 0 : tokens(u)],
                lhsT=w2c[:, col : col + P].bitcast(FP8X4),
                lhsT_scale=w2s[:, col : col + P],
                rhs=xc[u][0][:].bitcast(FP8X4),
                rhs_scale=xc[u][1][:],
                start=True,
                stop=True,
            )

        def st_e(u, t):
            s, n_tok = UNITS[u][1], tokens(u)
            if t == 0:
                hp[u] = hpp.tile([P, 4 * n_tok], BF16, name="hp", tag="hp")
            col = 4 * (4 if s == 3 else s) + t
            if t == 3 and u % 4 == 0 and 6 < u < NU - 11:
                nc.vector.tensor_scalar(
                    out=hp[u][:, n_tok * t : n_tok * (t + 1)],
                    in0=hps[u, t][:, 0:n_tok],
                    scalar1=bias2[:, col : col + 1],
                    scalar2=0.0,
                    op0=ALU.add,
                    op1=ALU.max,
                )
                return
            nc.scalar.activation(
                out=hp[u][:, n_tok * t : n_tok * (t + 1)],
                in_=hps[u, t][:, 0:n_tok],
                func=ACT.Relu,
                bias=bias2[:, col : col + 1],
                scale=1.0,
            )

        def st_f(u):
            hq[u] = hpp.tile([P, 4 * tokens(u)], BF16, name="hq", tag="hq", align_bytes=256)
            nc.vector.tensor_copy(
                out=hq[u][:].rearrange("p (c i t) -> p c t i", i=4, t=4),
                in_=hp[u][:].rearrange("p (t c i) -> p c t i", t=4, i=4),
            )

        def st_g(u):
            r, s, j0, nj = UNITS[u]
            codes = hcp.tile([P, tokens(u)], U32, name="hc%d" % s, tag="hc%d" % s, align_bytes=256)
            scales = hcp.tile([P, tokens(u)], U8, name="hs%d" % s, tag="hs%d" % s, align_bytes=256)
            for j in range(nj):
                hc[r, s, j0 + j] = (codes[:, P * j : P * (j + 1)], scales[:, P * j : P * (j + 1)])
            nc.vector.quantize_mx(out=codes[:].bitcast(FP8X4), scales=scales[:], in_=hq[u][:])

        def l2_pass(dst, r, s, j, blk, start, stop):
            nc.tensor.matmul_mx(
                out=dst,
                lhsT=hc[r, s, j][0].bitcast(FP8X4),
                lhsT_scale=hc[r, s, j][1],
                rhs=w3c[:, S * blk : S * (blk + 1)].bitcast(FP8X4),
                rhs_scale=w3s[:, S * blk : S * (blk + 1)],
                start=start,
                stop=stop,
            )

        def st_h(r, j):
            ops[r, j] = ps_o.tile([P, 4 * S], F32, name="ops", tag="ops")
            for a in range(A):
                dst = ops[r, j][:, S * a : S * (a + 1)]
                if is_full(r, j):
                    l2_pass(dst, r, 3, j, 3, True, False)
                    l2_pass(dst, r, 3, j, 7, False, False)
                    for b in range(A):
                        l2_pass(dst, r, b, j, b if b == a else 4 + b, False, b == A - 1)
                else:
                    l2_pass(dst, r, a, j, a, True, True)
            if not is_full(r, j):
                dst = ops[r, j][:, S * A :]
                l2_pass(dst, r, 3, j, 3, True, False)
                l2_pass(dst, r, 3, j, 7, False, False)
                for a in range(A):
                    l2_pass(dst, r, a, j, 4 + a, False, a == A - 1)

        end_bank = {}

        def st_h_open():
            r, j = NR - 1, NJ - 1
            for a in range(A):
                if a == 2:
                    end_bank[a] = ps_o.tile([P, 4 * S], F32, name="end", tag="ops")
                else:
                    end_bank[a] = ps_x.tile([P, 512], F32, name="end", tag="xt")
                dst = end_bank[a][:, 0:S]
                l2_pass(dst, r, 3, j, 3, True, False)
                l2_pass(dst, r, 3, j, 7, False, False)
                for b in range(A - 1):
                    l2_pass(dst, r, b, j, b if b == a else 4 + b, False, False)

        def st_h_close():
            r, j, b = NR - 1, NJ - 1, A - 1
            for a in range(A):
                l2_pass(end_bank[a][:, 0:S], r, b, j, b if b == a else 4 + b, False, True)

        def st_i1(r, j):
            if is_full(r, j):
                return
            esb[r, j] = outp.tile([P, A * S], F32, name="esb", tag="esb")
            nc.vector.scalar_tensor_tensor(
                out=esb[r, j][:].rearrange("p (a s) -> p a s", a=A),
                in0=ops[r, j][:, S * A :].unsqueeze(1).to_broadcast([P, A, S]),
                scalar=1.0 / 3.0,
                in1=beta[:].rearrange("p (a s) -> p a s", a=A),
                op0=ALU.mult,
                op1=ALU.add,
            )

        def out_rows(r):
            return out[RT * r : RT * (r + 1)].rearrange("(p j) a s -> p j (a s)", j=NJ)

        def st_i2(r, j):
            if j == 0:
                osb[r] = outp.tile([P, NJ * A * S], F32, name="osb", tag="osb")
            full = is_full(r, j)
            nc.vector.scalar_tensor_tensor(
                out=osb[r][:, A * S * j : A * S * (j + 1)],
                in0=ops[r, j][:, 0 : A * S],
                scalar=1.0 / 3.0 if full else 0.5,
                in1=beta[:] if full else esb[r, j][:],
                op0=ALU.mult,
                op1=ALU.add,
            )
            if r == NR - 1:
                store(r, j, 1)
            elif j == NJ - 1:
                store(r, 0, NJ)

        def store(r, j, n):
            nc.sync.dma_start(
                out=out_rows(r)[:, j : j + n, :],
                in_=osb[r][:, A * S * j : A * S * (j + n)].rearrange("p (j x) -> p j x", j=n),
            )

        def st_i_end():
            r, j = NR - 1, NJ - 1
            for a in range(A):
                nc.vector.scalar_tensor_tensor(
                    out=osb[r][:, A * S * j + S * a : A * S * j + S * (a + 1)],
                    in0=end_bank[a][:, 0:S],
                    scalar=1.0 / 3.0,
                    in1=beta[:, S * a : S * (a + 1)],
                    op0=ALU.mult,
                    op1=ALU.add,
                )
            store(r, j, 1)

        def setup_beta():
            pb = ps_o.tile([P, 4 * S], F32, name="pb", tag="ops")
            dst = pb[:, 0 : A * S]
            nc.tensor.matmul(out=dst, lhsT=threes[:], rhs=zrow[:, 0 : A * S], start=True, stop=False)
            for b in range(A + 1):
                nc.tensor.matmul(
                    out=dst,
                    lhsT=(minus if b < A else threes)[:],
                    rhs=zrow[:, S * b : S * (b + 1)].unsqueeze(1).to_broadcast([P, A, S]),
                    start=False,
                    stop=b == A,
                )
            nc.vector.tensor_scalar(
                out=beta[:], in0=dst, scalar1=1.0 / 3.0, scalar2=0.0, op0=ALU.mult, op1=ALU.add
            )

        w3g = const.tile([P, 8 * 4 * S], BF16, name="w3g", align_bytes=256)

        def prep_w3_first():
            for s in range(NS):
                nc.vector.tensor_scalar(
                    out=w3g[:, 4 * S * s : 4 * S * (s + 1)].rearrange("p (c i t) -> p c t i", i=4, t=4),
                    in0=w3raw[:, 4 * S * s : 4 * S * (s + 1)].rearrange("p (t c i) -> p c t i", t=4, i=4),
                    scalar1=2.0,
                    scalar2=0.0,
                    op0=ALU.mult,
                    op1=ALU.add,
                )

        def prep_w3_rest():
            for lo, hi, src_lo, factor in ((4, 7, 0, -0.5), (7, 8, 3, 0.5)):
                nc.vector.tensor_scalar(
                    out=w3g[:, 4 * S * lo : 4 * S * hi],
                    in0=w3g[:, 4 * S * src_lo : 4 * S * (src_lo + hi - lo)],
                    scalar1=factor,
                    scalar2=0.0,
                    op0=ALU.mult,
                    op1=ALU.add,
                )

        ready = []
        h_done = []
        state = {"a": 2, "b": 2, "c": 2, "h": 0, "i": 0}
        count = {}

        def quantise_h(u, n):
            st_g(u)
            r, s, j0, nj = UNITS[u]
            for j in range(j0, j0 + nj):
                count[r, j] = count.get((r, j), 0) + 1
                if count[r, j] == NS and (r, j) != (NR - 1, NJ - 1):
                    ready.append((r, j, n))

        def try_h(n):
            if state["h"] < len(ready) and ready[state["h"]][2] <= n - 1:
                r, j = ready[state["h"]][0:2]
                state["h"] += 1
                st_h(r, j)
                h_done.append((r, j, n))

        def pop_i(n):
            if state["i"] < len(h_done) and h_done[state["i"]][2] <= n - 1:
                state["i"] += 1
                return h_done[state["i"] - 1]
            return None

        def both_a(u):
            for hf in range(halves(u)):
                st_a(u, hf)
            r = UNITS[u][0]
            if u + 1 < NU and UNITS[u + 1][0] > r and r + 3 < NR:
                load_g(r + 3)
                if r + 3 > 3:
                    load_h(r + 3)

        def both_b(u, vector):
            for hf in range(halves(u)):
                if b_on_vector(u, hf) == vector:
                    st_b(u, hf)

        ctx.enter_context(pinned)
        both_a(0)
        both_a(1)
        wg3 = prep_w2(3)
        nc.vector.tensor_copy(out=bias2[:, 16:20], in_=bz[:, 16:20])
        nc.vector.tensor_copy(out=bias2[:, 0:12], in_=bz[:, 0:12])
        both_b(0, False)
        both_b(1, False)
        quant_w2(3, wg3)
        st_c(0)
        for t in range(4):
            st_d(0, t)
        st_c(1)
        wg = {0: prep_w2(0)}
        for n in range(NU + 1):
            lead = 2 if n < 4 else 3
            first_b = state["b"]
            while state["a"] < min(NU, n + lead + 1):
                both_a(state["a"])
                state["a"] += 1
            if n >= 5:
                st_f(n - 1)
            while state["c"] < first_b:
                st_c(state["c"])
                state["c"] += 1
            if n < 3:
                quant_w2(n, wg[n])
                if n < 2:
                    wg[n + 1] = prep_w2(n + 1)
            if n == 5:
                prep_w3_rest()
            if n == NU - 1:
                st_h_open()
            for t in range(4):
                if n < NU:
                    st_e(n, t)
                if n + 1 < NU:
                    st_d(n + 1, t)
                if t == (1 if n < NU - 4 else 3):
                    try_h(n)
            for u in range(first_b, state["a"]):
                both_b(u, False)
            state["b"] = state["a"]
            chunk = pop_i(n)
            if 1 <= n < 5:
                st_f(n - 1)
            if n == 5:
                nc.vector.quantize_mx(out=w3c[:].bitcast(FP8X4), scales=w3s[:], in_=w3g[:])
            if n == 5:
                setup_beta()
            if n == 3:
                prep_w3_first()
            if chunk:
                st_i1(chunk[0], chunk[1])
            if n >= 1:
                quantise_h(n - 1, n)
            if chunk:
                st_i2(chunk[0], chunk[1])
            for u in range(first_b, state["b"]):
                both_b(u, True)
        st_h_close()
        n = NU + 1
        while state["i"] < B // P - 1:
            try_h(n)
            chunk = pop_i(n)
            if chunk:
                st_i1(chunk[0], chunk[1])
                st_i2(chunk[0], chunk[1])
            n += 1
        st_i_end()
